import numpy as np
import ml_dtypes


def mxq(x, axis, fmt="e4m3"):
    dtype, down = {"e4m3": (ml_dtypes.float8_e4m3fn, 7), "e5m2": (ml_dtypes.float8_e5m2, 14)}[fmt]
    v = np.moveaxis(np.asarray(x, np.float32).astype(ml_dtypes.bfloat16).astype(np.float64), axis, -1)
    blocks = v.reshape(v.shape[:-1] + (-1, 32))
    amax = np.abs(blocks).max(-1, keepdims=True)
    byte = np.maximum(np.where(amax > 0, np.frexp(amax)[1] - 1 + 127, 0) - down, 1)
    scale = np.exp2(byte - 127.0)
    codes = (blocks / scale).astype(np.float32).astype(dtype).astype(np.float64)
    return np.moveaxis((codes * scale).reshape(v.shape), -1, axis)


WIDE = False


def mx_kscale(k):
    if not WIDE:
        return np.ones(k)
    levels = np.array([10, -10, 5, -5, 0])
    if k % 512:
        return np.exp2(np.random.permutation(np.resize(levels, k // 32))).repeat(32)
    a = np.empty((k // 512, 16))
    for p in range(k // 512):
        a[p, :8] = np.random.permutation(np.resize(levels, 8))
        for g in range(8):
            far = levels[np.abs(levels - a[p, g]) >= 10]
            a[p, g + 8] = far[np.random.randint(len(far))]
    return np.exp2(a.ravel()).repeat(32)


BF16 = ml_dtypes.bfloat16


def bf(x):
    return np.asarray(x, np.float32).astype(BF16)


def f64(x):
    return np.asarray(x).astype(np.float64)


T, K, E, H, KVH, D = 128, 1024, 512, 16, 4, 128
EPS = 1e-05


def rmsnorm(x, w):
    var = np.mean(np.square(x), axis=-1, keepdims=True)
    return x * (1.0 / np.sqrt(var + EPS)) * w


def setup_inputs():
    s = mx_kscale(E)
    return {"hidden_states": bf(np.random.standard_normal((T, E)) * s),
            "Wq": bf(np.random.standard_normal((H * D, E)) / np.sqrt(E) / s),
            "q_norm_w": bf(1.5 + 0.1 * np.random.standard_normal(D))}


def reference(hidden_states, Wq, q_norm_w):
    q = mxq(f64(hidden_states), 1, "e4m3") @ mxq(f64(Wq), 1, "e4m3").T
    qh = rmsnorm(q.reshape(T, H, D), f64(q_norm_w))
    return qh.transpose(1, 0, 2)

@@ -1,0 +1,151 @@
+from contextlib import ExitStack
+
+import concourse.masks as masks
+import concourse.mybir as mybir
+
+F32 = mybir.dt.float32
+BF16 = mybir.dt.bfloat16
+U32 = mybir.dt.uint32
+U8 = mybir.dt.uint8
+FP8X4 = mybir.dt.float8_e4m3fn_x4
+ACT = mybir.ActivationFunctionType
+ALU = mybir.AluOpType
+
+P = 128
+TOKENS = 128
+K = 512
+HEADS = 16
+HEAD_DIM = 128
+EPS = 1e-05
+
+K_WORDS = K // 2
+HALVES = K_WORDS // P
+PACK = 4
+PIECE = 256
+N_PIECES = HEADS * HEAD_DIM // PIECE
+ROWS = PIECE // P
+HEADS_PER_PIECE = PIECE // HEAD_DIM
+VECTOR_EVERY = 3
+
+FLOPS = 2 * TOKENS * HEADS * HEAD_DIM * K
+
+
+def tile_combcrossattention_pa_s_kernel(tc, hidden_states, Wq, q_norm_w, out):
+    nc = tc.nc
+    with ExitStack() as ctx:
+        consts = ctx.enter_context(tc.tile_pool(name="consts", bufs=1))
+        pieces = ctx.enter_context(tc.tile_pool(name="pieces", bufs=N_PIECES))
+        flipped = ctx.enter_context(tc.psum_pool(name="flipped", bufs=4))
+        sums = ctx.enter_context(tc.psum_pool(name="sums", bufs=4))
+
+        def load_piece(i):
+            raw = pieces.tile([P, ROWS * K], BF16, name="w_raw")
+            rows = Wq[i * PIECE : (i + 1) * PIECE, :]
+            nc.sync.dma_start(out=raw[:], in_=rows.rearrange("(p a) k -> p (a k)", a=ROWS))
+            return raw
+
+        w_raw = [load_piece(0)]
+        hs_raw = consts.tile([P, K], BF16)
+        nc.sync.dma_start(out=hs_raw[:], in_=hidden_states)
+        gain_row = consts.tile([P, HEAD_DIM], BF16)
+        nc.vector.memset(gain_row[:], 0.0)
+        nc.sync.dma_start(out=gain_row[0:1, :], in_=q_norm_w.rearrange("(o d) -> o d", o=1))
+        for i in range(1, N_PIECES):
+            w_raw.append(load_piece(i))
+
+        ident = consts.tile([P, P], F32)
+        masks.make_identity(nc, ident[:])
+        ones = consts.tile([P, P], BF16)
+        nc.vector.memset(ones[:], 1.0)
+        one = consts.tile([P, 1], F32)
+        nc.vector.memset(one[:], 1.0)
+        nc.scalar.activation(out=one[:], in_=one[:], func=ACT.Abs_reciprocal_sqrt)
+
+        def transpose_words(dst, src_words):
+            for u in range(HALVES):
+                nc.tensor.transpose(dst[:, u, :], src_words[:, u::HALVES], ident[:])
+
+        def flip(i):
+            words = w_raw[i][:].bitcast(F32)
+            bank = flipped.tile([P, ROWS, HALVES, P], F32, name="bank", tag="bank")
+            for a in range(ROWS):
+                transpose_words(bank[:, a], words[:, a * K_WORDS : (a + 1) * K_WORDS])
+            return bank
+
+        bank_of = {0: flip(0)}
+
+        hs_flipped = flipped.tile([P, HALVES, TOKENS], F32, name="hs_flipped", tag="bank")
+        transpose_words(hs_flipped, hs_raw[:].bitcast(F32))
+        hs_grouped = consts.tile([P, TOKENS * PACK], BF16, align_bytes=64)
+        nc.vector.tensor_copy(
+            out=hs_grouped[:].bitcast(F32).rearrange("p (r u) -> p r u", u=HALVES),
+            in_=hs_flipped[:].rearrange("p u r -> p r u"),
+        )
+        hs_codes = consts.tile([P, TOKENS], U32, align_bytes=64)
+        hs_scales = consts.tile([P, TOKENS], U8, align_bytes=64)
+        nc.vector.quantize_mx(out=hs_codes[:].bitcast(FP8X4), scales=hs_scales[:], in_=hs_grouped[:])
+
+        gain_spread = flipped.tile([P, HEAD_DIM], F32, name="gain_spread", tag="bank")
+        nc.tensor.matmul(out=gain_spread[:], lhsT=ones[:], rhs=gain_row[:], start=True, stop=True)
+        gain = consts.tile([P, HEAD_DIM], F32)
+        nc.vector.tensor_copy(out=gain[:], in_=gain_spread[:])
+
+        for i in range(N_PIECES):
+            if i + 1 < N_PIECES:
+                bank_of[i + 1] = flip(i + 1)
+
+            grouped = pieces.tile([P, PIECE * PACK], BF16, align_bytes=64, name="grouped")
+            dst = grouped[:].bitcast(F32).rearrange("p (a c u) -> p a c u", a=ROWS, u=HALVES)
+            src = bank_of[i][:].rearrange("p a u c -> p a c u")
+            if i % VECTOR_EVERY == 1:
+                nc.vector.tensor_copy(out=dst, in_=src)
+            else:
+                nc.scalar.copy(out=dst, in_=src)
+
+            codes = pieces.tile([P, PIECE], U32, align_bytes=64, name="codes")
+            scales = pieces.tile([P, PIECE], U8, align_bytes=64, name="scales")
+            nc.vector.quantize_mx(out=codes[:].bitcast(FP8X4), scales=scales[:], in_=grouped[:])
+
+            acc = sums.tile([TOKENS, PIECE], F32, name="acc")
+            nc.tensor.matmul_mx(
+                out=acc[:],
+                lhsT=hs_codes[:].bitcast(FP8X4),
+                lhsT_scale=hs_scales[:],
+                rhs=codes[:].bitcast(FP8X4),
+                rhs_scale=scales[:],
+                start=True,
+                stop=True,
+            )
+
+            squares = pieces.tile([TOKENS, HEADS_PER_PIECE, ROWS, P // ROWS], F32, name="squares")
+            sumsq = pieces.tile([TOKENS, HEADS_PER_PIECE], F32, name="sumsq")
+            acc_heads = acc[:].rearrange("t (a h c) -> t h a c", a=ROWS, h=HEADS_PER_PIECE)
+            for h in range(HEADS_PER_PIECE):
+                nc.scalar.activation(
+                    out=squares[:, h],
+                    in_=acc_heads[:, h],
+                    func=ACT.Square,
+                    accum_out=sumsq[:, h : h + 1],
+                )
+            inv_rms = pieces.tile([TOKENS, HEADS_PER_PIECE], F32, name="inv_rms")
+            nc.scalar.activation(
+                out=inv_rms[:],
+                in_=sumsq[:],
+                func=ACT.Abs_reciprocal_sqrt,
+                scale=1.0 / HEAD_DIM,
+                bias=EPS,
+            )
+
+            normed = pieces.tile([TOKENS, HEADS_PER_PIECE, HEAD_DIM], F32, name="normed")
+            acc_by_d = acc[:].rearrange("t (a h c) -> t h c a", a=ROWS, h=HEADS_PER_PIECE)
+            for h in range(HEADS_PER_PIECE):
+                nc.vector.scalar_tensor_tensor(
+                    out=normed[:, h, :].rearrange("t (c a) -> t c a", a=ROWS),
+                    in0=acc_by_d[:, h],
+                    scalar=inv_rms[:, h : h + 1],
+                    in1=gain[:].rearrange("t (c a) -> t c a", a=ROWS),
+                    op0=ALU.mult,
+                    op1=ALU.mult,
+                )
+            heads = out[i * HEADS_PER_PIECE : (i + 1) * HEADS_PER_PIECE]
+            nc.sync.dma_start(out=heads.rearrange("h t d -> t h d"), in_=normed[:])

@@ -25,6 +25,7 @@ PIECE = 256
 N_PIECES = HEADS * HEAD_DIM // PIECE
 ROWS = PIECE // P
 HEADS_PER_PIECE = PIECE // HEAD_DIM
+GROUP = 2
 VECTOR_EVERY = 3
 
 FLOPS = 2 * TOKENS * HEADS * HEAD_DIM * K
@@ -72,40 +73,23 @@ def tile_combcrossattention_pa_s_kernel(tc, hidden_states, Wq, q_norm_w, out):
                 transpose_words(bank[:, a], words[:, a * K_WORDS : (a + 1) * K_WORDS])
             return bank
 
-        bank_of = {0: flip(0)}
-
-        hs_flipped = flipped.tile([P, HALVES, TOKENS], F32, name="hs_flipped", tag="bank")
-        transpose_words(hs_flipped, hs_raw[:].bitcast(F32))
-        hs_grouped = consts.tile([P, TOKENS * PACK], BF16, align_bytes=64)
-        nc.vector.tensor_copy(
-            out=hs_grouped[:].bitcast(F32).rearrange("p (r u) -> p r u", u=HALVES),
-            in_=hs_flipped[:].rearrange("p u r -> p r u"),
-        )
-        hs_codes = consts.tile([P, TOKENS], U32, align_bytes=64)
-        hs_scales = consts.tile([P, TOKENS], U8, align_bytes=64)
-        nc.vector.quantize_mx(out=hs_codes[:].bitcast(FP8X4), scales=hs_scales[:], in_=hs_grouped[:])
-
-        gain_spread = flipped.tile([P, HEAD_DIM], F32, name="gain_spread", tag="bank")
-        nc.tensor.matmul(out=gain_spread[:], lhsT=ones[:], rhs=gain_row[:], start=True, stop=True)
-        gain = consts.tile([P, HEAD_DIM], F32)
-        nc.vector.tensor_copy(out=gain[:], in_=gain_spread[:])
-
-        for i in range(N_PIECES):
-            if i + 1 < N_PIECES:
-                bank_of[i + 1] = flip(i + 1)
-
+        def copy_out(i, bank):
             grouped = pieces.tile([P, PIECE * PACK], BF16, align_bytes=64, name="grouped")
             dst = grouped[:].bitcast(F32).rearrange("p (a c u) -> p a c u", a=ROWS, u=HALVES)
-            src = bank_of[i][:].rearrange("p a u c -> p a c u")
+            src = bank[:].rearrange("p a u c -> p a c u")
             if i % VECTOR_EVERY == 1:
                 nc.vector.tensor_copy(out=dst, in_=src)
             else:
                 nc.scalar.copy(out=dst, in_=src)
+            return grouped
 
+        def quantise(grouped):
             codes = pieces.tile([P, PIECE], U32, align_bytes=64, name="codes")
             scales = pieces.tile([P, PIECE], U8, align_bytes=64, name="scales")
             nc.vector.quantize_mx(out=codes[:].bitcast(FP8X4), scales=scales[:], in_=grouped[:])
+            return codes, scales
 
+        def multiply(codes, scales):
             acc = sums.tile([TOKENS, PIECE], F32, name="acc")
             nc.tensor.matmul_mx(
                 out=acc[:],
@@ -116,7 +100,9 @@ def tile_combcrossattention_pa_s_kernel(tc, hidden_states, Wq, q_norm_w, out):
                 start=True,
                 stop=True,
             )
+            return acc
 
+        def norm(i, acc):
             squares = pieces.tile([TOKENS, HEADS_PER_PIECE, ROWS, P // ROWS], F32, name="squares")
             sumsq = pieces.tile([TOKENS, HEADS_PER_PIECE], F32, name="sumsq")
             acc_heads = acc[:].rearrange("t (a h c) -> t h a c", a=ROWS, h=HEADS_PER_PIECE)
@@ -149,3 +135,34 @@ def tile_combcrossattention_pa_s_kernel(tc, hidden_states, Wq, q_norm_w, out):
                 )
             heads = out[i * HEADS_PER_PIECE : (i + 1) * HEADS_PER_PIECE]
             nc.sync.dma_start(out=heads.rearrange("h t d -> t h d"), in_=normed[:])
+
+        ctx.enter_context(tc.manual_schedule(engines={mybir.EngineType.PE}))
+        banks = {0: flip(0)}
+
+        hs_flipped = flipped.tile([P, HALVES, TOKENS], F32, name="hs_flipped", tag="bank")
+        transpose_words(hs_flipped, hs_raw[:].bitcast(F32))
+        hs_grouped = consts.tile([P, TOKENS * PACK], BF16, align_bytes=64)
+        nc.vector.tensor_copy(
+            out=hs_grouped[:].bitcast(F32).rearrange("p (r u) -> p r u", u=HALVES),
+            in_=hs_flipped[:].rearrange("p u r -> p r u"),
+        )
+        hs_codes = consts.tile([P, TOKENS], U32, align_bytes=64)
+        hs_scales = consts.tile([P, TOKENS], U8, align_bytes=64)
+        nc.vector.quantize_mx(out=hs_codes[:].bitcast(FP8X4), scales=hs_scales[:], in_=hs_grouped[:])
+
+        gain_spread = flipped.tile([P, HEAD_DIM], F32, name="gain_spread", tag="bank")
+        nc.tensor.matmul(out=gain_spread[:], lhsT=ones[:], rhs=gain_row[:], start=True, stop=True)
+        gain = consts.tile([P, HEAD_DIM], F32)
+        nc.vector.tensor_copy(out=gain[:], in_=gain_spread[:])
+
+        for i in range(1, 2 * GROUP):
+            banks[i] = flip(i)
+        for first in range(0, N_PIECES, GROUP):
+            group = range(first, first + GROUP)
+            grouped = {i: copy_out(i, banks[i]) for i in group}
+            packed = {i: quantise(grouped[i]) for i in group}
+            accs = {i: multiply(*packed[i]) for i in group}
+            for i in range(first + 2 * GROUP, min(first + 3 * GROUP, N_PIECES)):
+                banks[i] = flip(i)
+            for i in group:
+                norm(i, accs[i])

@@ -26,7 +26,7 @@ N_PIECES = HEADS * HEAD_DIM // PIECE
 ROWS = PIECE // P
 HEADS_PER_PIECE = PIECE // HEAD_DIM
 GROUP = 2
-VECTOR_EVERY = 3
+VECTOR_PIECES = (3, 6)
 
 FLOPS = 2 * TOKENS * HEADS * HEAD_DIM * K
 
@@ -77,7 +77,7 @@ def tile_combcrossattention_pa_s_kernel(tc, hidden_states, Wq, q_norm_w, out):
             grouped = pieces.tile([P, PIECE * PACK], BF16, align_bytes=64, name="grouped")
             dst = grouped[:].bitcast(F32).rearrange("p (a c u) -> p a c u", a=ROWS, u=HALVES)
             src = bank[:].rearrange("p a u c -> p a c u")
-            if i % VECTOR_EVERY == 1:
+            if i in VECTOR_PIECES:
                 nc.vector.tensor_copy(out=dst, in_=src)
             else:
                 nc.scalar.copy(out=dst, in_=src)

@@ -21,28 +21,29 @@ EPS = 1e-05
 K_WORDS = K // 2
 HALVES = K_WORDS // P
 PACK = 4
-PIECE = 256
-N_PIECES = HEADS * HEAD_DIM // PIECE
-ROWS = PIECE // P
-HEADS_PER_PIECE = PIECE // HEAD_DIM
-GROUP = 2
-VECTOR_PIECES = (3, 6)
+SIZES = 7 * [256] + 2 * [128]
+FLIP_RUNS = (4, 4)
+PASS_RUNS = (3, 6)
+VECTOR_PIECES = (4, 5, 8)
 
 FLOPS = 2 * TOKENS * HEADS * HEAD_DIM * K
 
 
 def tile_combcrossattention_pa_s_kernel(tc, hidden_states, Wq, q_norm_w, out):
     nc = tc.nc
+    n = len(SIZES)
+    starts = [sum(SIZES[:i]) for i in range(n)]
     with ExitStack() as ctx:
         consts = ctx.enter_context(tc.tile_pool(name="consts", bufs=1))
-        pieces = ctx.enter_context(tc.tile_pool(name="pieces", bufs=N_PIECES))
+        pieces = ctx.enter_context(tc.tile_pool(name="pieces", bufs=n))
         flipped = ctx.enter_context(tc.psum_pool(name="flipped", bufs=4))
         sums = ctx.enter_context(tc.psum_pool(name="sums", bufs=4))
 
         def load_piece(i):
-            raw = pieces.tile([P, ROWS * K], BF16, name="w_raw")
-            rows = Wq[i * PIECE : (i + 1) * PIECE, :]
-            nc.sync.dma_start(out=raw[:], in_=rows.rearrange("(p a) k -> p (a k)", a=ROWS))
+            rows = SIZES[i] // P
+            raw = pieces.tile([P, rows * K], BF16, name="w_raw")
+            src = Wq[starts[i] : starts[i] + SIZES[i], :]
+            nc.sync.dma_start(out=raw[:], in_=src.rearrange("(p a) k -> p (a k)", a=rows))
             return raw
 
         w_raw = [load_piece(0)]
@@ -51,7 +52,7 @@ def tile_combcrossattention_pa_s_kernel(tc, hidden_states, Wq, q_norm_w, out):
         gain_row = consts.tile([P, HEAD_DIM], BF16)
         nc.vector.memset(gain_row[:], 0.0)
         nc.sync.dma_start(out=gain_row[0:1, :], in_=q_norm_w.rearrange("(o d) -> o d", o=1))
-        for i in range(1, N_PIECES):
+        for i in range(1, n):
             w_raw.append(load_piece(i))
 
         ident = consts.tile([P, P], F32)
@@ -68,14 +69,16 @@ def tile_combcrossattention_pa_s_kernel(tc, hidden_states, Wq, q_norm_w, out):
 
         def flip(i):
             words = w_raw[i][:].bitcast(F32)
-            bank = flipped.tile([P, ROWS, HALVES, P], F32, name="bank", tag="bank")
-            for a in range(ROWS):
+            rows = SIZES[i] // P
+            bank = flipped.tile([P, rows, HALVES, P], F32, name="bank", tag="bank")
+            for a in range(rows):
                 transpose_words(bank[:, a], words[:, a * K_WORDS : (a + 1) * K_WORDS])
             return bank
 
         def copy_out(i, bank):
-            grouped = pieces.tile([P, PIECE * PACK], BF16, align_bytes=64, name="grouped")
-            dst = grouped[:].bitcast(F32).rearrange("p (a c u) -> p a c u", a=ROWS, u=HALVES)
+            rows = SIZES[i] // P
+            grouped = pieces.tile([P, SIZES[i] * PACK], BF16, align_bytes=64, name="grouped")
+            dst = grouped[:].bitcast(F32).rearrange("p (a c u) -> p a c u", a=rows, u=HALVES)
             src = bank[:].rearrange("p a u c -> p a c u")
             if i in VECTOR_PIECES:
                 nc.vector.tensor_copy(out=dst, in_=src)
@@ -83,14 +86,14 @@ def tile_combcrossattention_pa_s_kernel(tc, hidden_states, Wq, q_norm_w, out):
                 nc.scalar.copy(out=dst, in_=src)
             return grouped
 
-        def quantise(grouped):
-            codes = pieces.tile([P, PIECE], U32, align_bytes=64, name="codes")
-            scales = pieces.tile([P, PIECE], U8, align_bytes=64, name="scales")
+        def quantise(i, grouped):
+            codes = pieces.tile([P, SIZES[i]], U32, align_bytes=64, name="codes")
+            scales = pieces.tile([P, SIZES[i]], U8, align_bytes=64, name="scales")
             nc.vector.quantize_mx(out=codes[:].bitcast(FP8X4), scales=scales[:], in_=grouped[:])
             return codes, scales
 
-        def multiply(codes, scales):
-            acc = sums.tile([TOKENS, PIECE], F32, name="acc")
+        def multiply(i, codes, scales):
+            acc = sums.tile([TOKENS, SIZES[i]], F32, name="acc")
             nc.tensor.matmul_mx(
                 out=acc[:],
                 lhsT=hs_codes[:].bitcast(FP8X4),
@@ -103,17 +106,19 @@ def tile_combcrossattention_pa_s_kernel(tc, hidden_states, Wq, q_norm_w, out):
             return acc
 
         def norm(i, acc):
-            squares = pieces.tile([TOKENS, HEADS_PER_PIECE, ROWS, P // ROWS], F32, name="squares")
-            sumsq = pieces.tile([TOKENS, HEADS_PER_PIECE], F32, name="sumsq")
-            acc_heads = acc[:].rearrange("t (a h c) -> t h a c", a=ROWS, h=HEADS_PER_PIECE)
-            for h in range(HEADS_PER_PIECE):
+            rows = SIZES[i] // P
+            heads = SIZES[i] // HEAD_DIM
+            squares = pieces.tile([TOKENS, heads, rows, P // rows], F32, name="squares")
+            sumsq = pieces.tile([TOKENS, heads], F32, name="sumsq")
+            acc_heads = acc[:].rearrange("t (a h c) -> t h a c", a=rows, h=heads)
+            for h in range(heads):
                 nc.scalar.activation(
                     out=squares[:, h],
                     in_=acc_heads[:, h],
                     func=ACT.Square,
                     accum_out=sumsq[:, h : h + 1],
                 )
-            inv_rms = pieces.tile([TOKENS, HEADS_PER_PIECE], F32, name="inv_rms")
+            inv_rms = pieces.tile([TOKENS, heads], F32, name="inv_rms")
             nc.scalar.activation(
                 out=inv_rms[:],
                 in_=sumsq[:],
@@ -122,19 +127,19 @@ def tile_combcrossattention_pa_s_kernel(tc, hidden_states, Wq, q_norm_w, out):
                 bias=EPS,
             )
 
-            normed = pieces.tile([TOKENS, HEADS_PER_PIECE, HEAD_DIM], F32, name="normed")
-            acc_by_d = acc[:].rearrange("t (a h c) -> t h c a", a=ROWS, h=HEADS_PER_PIECE)
-            for h in range(HEADS_PER_PIECE):
+            normed = pieces.tile([TOKENS, heads, HEAD_DIM], F32, name="normed")
+            acc_by_d = acc[:].rearrange("t (a h c) -> t h c a", a=rows, h=heads)
+            for h in range(heads):
                 nc.vector.scalar_tensor_tensor(
-                    out=normed[:, h, :].rearrange("t (c a) -> t c a", a=ROWS),
+                    out=normed[:, h, :].rearrange("t (c a) -> t c a", a=rows),
                     in0=acc_by_d[:, h],
                     scalar=inv_rms[:, h : h + 1],
-                    in1=gain[:].rearrange("t (c a) -> t c a", a=ROWS),
+                    in1=gain[:].rearrange("t (c a) -> t c a", a=rows),
                     op0=ALU.mult,
                     op1=ALU.mult,
                 )
-            heads = out[i * HEADS_PER_PIECE : (i + 1) * HEADS_PER_PIECE]
-            nc.sync.dma_start(out=heads.rearrange("h t d -> t h d"), in_=normed[:])
+            first = starts[i] // HEAD_DIM
+            nc.sync.dma_start(out=out[first : first + heads].rearrange("h t d -> t h d"), in_=normed[:])
 
         ctx.enter_context(tc.manual_schedule(engines={mybir.EngineType.PE}))
         banks = {0: flip(0)}
@@ -155,14 +160,22 @@ def tile_combcrossattention_pa_s_kernel(tc, hidden_states, Wq, q_norm_w, out):
         gain = consts.tile([P, HEAD_DIM], F32)
         nc.vector.tensor_copy(out=gain[:], in_=gain_spread[:])
 
-        for i in range(1, 2 * GROUP):
-            banks[i] = flip(i)
-        for first in range(0, N_PIECES, GROUP):
-            group = range(first, first + GROUP)
-            grouped = {i: copy_out(i, banks[i]) for i in group}
-            packed = {i: quantise(grouped[i]) for i in group}
-            accs = {i: multiply(*packed[i]) for i in group}
-            for i in range(first + 2 * GROUP, min(first + 3 * GROUP, N_PIECES)):
+
+        grouped = {0: copy_out(0, banks[0])}
+        packed = {}
+        accs = {}
+        done = 0
+        flipped_to = 1
+        for flip_run, pass_run in zip(FLIP_RUNS, PASS_RUNS):
+            for i in range(flipped_to, flipped_to + flip_run):
                 banks[i] = flip(i)
+                grouped[i] = copy_out(i, banks[i])
+            flipped_to += flip_run
+            group = range(done, done + pass_run)
+            for i in group:
+                packed[i] = quantise(i, grouped[i])
+            for i in group:
+                accs[i] = multiply(i, *packed[i])
             for i in group:
                 norm(i, accs[i])
+            done += pass_run

@@ -24,6 +24,7 @@ PACK = 4
 SIZES = 7 * [256] + 2 * [128]
 FLIP_RUNS = (4, 4)
 PASS_RUNS = (3, 6)
+WARM_PASSES = 10
 VECTOR_PIECES = (4, 5, 8)
 
 FLOPS = 2 * TOKENS * HEADS * HEAD_DIM * K
@@ -38,6 +39,15 @@ def tile_combcrossattention_pa_s_kernel(tc, hidden_states, Wq, q_norm_w, out):
         pieces = ctx.enter_context(tc.tile_pool(name="pieces", bufs=n))
         flipped = ctx.enter_context(tc.psum_pool(name="flipped", bufs=4))
         sums = ctx.enter_context(tc.psum_pool(name="sums", bufs=4))
+
+        idle_grouped = consts.tile([P, P * PACK], BF16, align_bytes=64)
+        nc.vector.memset(idle_grouped[:].bitcast(F32), 0.0)
+        idle_codes = consts.tile([P, P], U32, align_bytes=64)
+        idle_scales = consts.tile([P, P], U8, align_bytes=64)
+        nc.vector.quantize_mx(
+            out=idle_codes[:].bitcast(FP8X4), scales=idle_scales[:], in_=idle_grouped[:]
+        )
+        idle_sums = sums.tile([P, P], F32, name="idle_sums", tag="acc")
 
         def load_piece(i):
             rows = SIZES[i] // P
@@ -142,6 +152,16 @@ def tile_combcrossattention_pa_s_kernel(tc, hidden_states, Wq, q_norm_w, out):
             nc.sync.dma_start(out=out[first : first + heads].rearrange("h t d -> t h d"), in_=normed[:])
 
         ctx.enter_context(tc.manual_schedule(engines={mybir.EngineType.PE}))
+        for w in range(WARM_PASSES):
+            nc.tensor.matmul_mx(
+                out=idle_sums[:],
+                lhsT=idle_codes[:].bitcast(FP8X4),
+                lhsT_scale=idle_scales[:],
+                rhs=idle_codes[:].bitcast(FP8X4),
+                rhs_scale=idle_scales[:],
+                start=True,
+                stop=True,
+            )
         banks = {0: flip(0)}
 
         hs_flipped = flipped.tile([P, HALVES, TOKENS], F32, name="hs_flipped", tag="bank")

@@ -22,10 +22,8 @@ K_WORDS = K // 2
 HALVES = K_WORDS // P
 PACK = 4
 SIZES = 7 * [256] + 2 * [128]
-FLIP_RUNS = (4, 4)
-PASS_RUNS = (3, 6)
 WARM_PASSES = 10
-VECTOR_PIECES = (4, 5, 8)
+VECTOR_PIECES = (4, 7, 8)
 
 FLOPS = 2 * TOKENS * HEADS * HEAD_DIM * K
 
@@ -37,8 +35,7 @@ def tile_combcrossattention_pa_s_kernel(tc, hidden_states, Wq, q_norm_w, out):
     with ExitStack() as ctx:
         consts = ctx.enter_context(tc.tile_pool(name="consts", bufs=1))
         pieces = ctx.enter_context(tc.tile_pool(name="pieces", bufs=n))
-        flipped = ctx.enter_context(tc.psum_pool(name="flipped", bufs=4))
-        sums = ctx.enter_context(tc.psum_pool(name="sums", bufs=4))
+        banked = ctx.enter_context(tc.psum_pool(name="banked", bufs=8))
 
         idle_grouped = consts.tile([P, P * PACK], BF16, align_bytes=64)
         nc.vector.memset(idle_grouped[:].bitcast(F32), 0.0)
@@ -47,7 +44,7 @@ def tile_combcrossattention_pa_s_kernel(tc, hidden_states, Wq, q_norm_w, out):
         nc.vector.quantize_mx(
             out=idle_codes[:].bitcast(FP8X4), scales=idle_scales[:], in_=idle_grouped[:]
         )
-        idle_sums = sums.tile([P, P], F32, name="idle_sums", tag="acc")
+        idle_sums = banked.tile([P, P], F32, name="idle_sums", tag="bank")
 
         def load_piece(i):
             rows = SIZES[i] // P
@@ -80,7 +77,7 @@ def tile_combcrossattention_pa_s_kernel(tc, hidden_states, Wq, q_norm_w, out):
         def flip(i):
             words = w_raw[i][:].bitcast(F32)
             rows = SIZES[i] // P
-            bank = flipped.tile([P, rows, HALVES, P], F32, name="bank", tag="bank")
+            bank = banked.tile([P, rows, HALVES, P], F32, name="bank", tag="bank")
             for a in range(rows):
                 transpose_words(bank[:, a], words[:, a * K_WORDS : (a + 1) * K_WORDS])
             return bank
@@ -103,7 +100,7 @@ def tile_combcrossattention_pa_s_kernel(tc, hidden_states, Wq, q_norm_w, out):
             return codes, scales
 
         def multiply(i, codes, scales):
-            acc = sums.tile([TOKENS, SIZES[i]], F32, name="acc")
+            acc = banked.tile([TOKENS, SIZES[i]], F32, name="acc", tag="bank")
             nc.tensor.matmul_mx(
                 out=acc[:],
                 lhsT=hs_codes[:].bitcast(FP8X4),
@@ -115,7 +112,7 @@ def tile_combcrossattention_pa_s_kernel(tc, hidden_states, Wq, q_norm_w, out):
             )
             return acc
 
-        def norm(i, acc):
+        def rms(i, acc):
             rows = SIZES[i] // P
             heads = SIZES[i] // HEAD_DIM
             squares = pieces.tile([TOKENS, heads, rows, P // rows], F32, name="squares")
@@ -136,7 +133,11 @@ def tile_combcrossattention_pa_s_kernel(tc, hidden_states, Wq, q_norm_w, out):
                 scale=1.0 / HEAD_DIM,
                 bias=EPS,
             )
+            return inv_rms
 
+        def scale(i, acc, inv_rms):
+            rows = SIZES[i] // P
+            heads = SIZES[i] // HEAD_DIM
             normed = pieces.tile([TOKENS, heads, HEAD_DIM], F32, name="normed")
             acc_by_d = acc[:].rearrange("t (a h c) -> t h c a", a=rows, h=heads)
             for h in range(heads):
@@ -151,7 +152,7 @@ def tile_combcrossattention_pa_s_kernel(tc, hidden_states, Wq, q_norm_w, out):
             first = starts[i] // HEAD_DIM
             nc.sync.dma_start(out=out[first : first + heads].rearrange("h t d -> t h d"), in_=normed[:])
 
-        ctx.enter_context(tc.manual_schedule(engines={mybir.EngineType.PE}))
+        ctx.enter_context(tc.manual_schedule())
         for w in range(WARM_PASSES):
             nc.tensor.matmul_mx(
                 out=idle_sums[:],
@@ -164,7 +165,7 @@ def tile_combcrossattention_pa_s_kernel(tc, hidden_states, Wq, q_norm_w, out):
             )
         banks = {0: flip(0)}
 
-        hs_flipped = flipped.tile([P, HALVES, TOKENS], F32, name="hs_flipped", tag="bank")
+        hs_flipped = banked.tile([P, HALVES, TOKENS], F32, name="hs_flipped", tag="bank")
         transpose_words(hs_flipped, hs_raw[:].bitcast(F32))
         hs_grouped = consts.tile([P, TOKENS * PACK], BF16, align_bytes=64)
         nc.vector.tensor_copy(
@@ -175,7 +176,7 @@ def tile_combcrossattention_pa_s_kernel(tc, hidden_states, Wq, q_norm_w, out):
         hs_scales = consts.tile([P, TOKENS], U8, align_bytes=64)
         nc.vector.quantize_mx(out=hs_codes[:].bitcast(FP8X4), scales=hs_scales[:], in_=hs_grouped[:])
 
-        gain_spread = flipped.tile([P, HEAD_DIM], F32, name="gain_spread", tag="bank")
+        gain_spread = banked.tile([P, HEAD_DIM], F32, name="gain_spread", tag="bank")
         nc.tensor.matmul(out=gain_spread[:], lhsT=ones[:], rhs=gain_row[:], start=True, stop=True)
         gain = consts.tile([P, HEAD_DIM], F32)
         nc.vector.tensor_copy(out=gain[:], in_=gain_spread[:])
@@ -184,18 +185,27 @@ def tile_combcrossattention_pa_s_kernel(tc, hidden_states, Wq, q_norm_w, out):
         grouped = {0: copy_out(0, banks[0])}
         packed = {}
         accs = {}
-        done = 0
-        flipped_to = 1
-        for flip_run, pass_run in zip(FLIP_RUNS, PASS_RUNS):
-            for i in range(flipped_to, flipped_to + flip_run):
-                banks[i] = flip(i)
-                grouped[i] = copy_out(i, banks[i])
-            flipped_to += flip_run
-            group = range(done, done + pass_run)
-            for i in group:
-                packed[i] = quantise(i, grouped[i])
-            for i in group:
-                accs[i] = multiply(i, *packed[i])
-            for i in group:
-                norm(i, accs[i])
-            done += pass_run
+        inv = {}
+        for i in range(1, 5):
+            banks[i] = flip(i)
+            grouped[i] = copy_out(i, banks[i])
+            packed[i - 1] = quantise(i - 1, grouped[i - 1])
+        packed[4] = quantise(4, grouped[4])
+        for i in range(3):
+            accs[i] = multiply(i, *packed[i])
+        for i in range(5, 9):
+            banks[i] = flip(i)
+        for i in range(3):
+            inv[i] = rms(i, accs[i])
+            if i < 2:
+                scale(i, accs[i], inv[i])
+        for i in range(5, 9):
+            grouped[i] = copy_out(i, banks[i])
+        scale(2, accs[2], inv[2])
+        for i in range(5, 9):
+            packed[i] = quantise(i, grouped[i])
+        for i in range(3, 9):
+            accs[i] = multiply(i, *packed[i])
+        for i in range(3, 9):
+            inv[i] = rms(i, accs[i])
+            scale(i, accs[i], inv[i])

@@ -23,7 +23,7 @@ HALVES = K_WORDS // P
 PACK = 4
 SIZES = 7 * [256] + 2 * [128]
 WARM_PASSES = 10
-VECTOR_PIECES = (4, 7, 8)
+VECTOR_PIECES = (4, 5, 7)
 
 FLOPS = 2 * TOKENS * HEADS * HEAD_DIM * K
 
@@ -112,34 +112,33 @@ def tile_combcrossattention_pa_s_kernel(tc, hidden_states, Wq, q_norm_w, out):
             )
             return acc
 
-        def rms(i, acc):
+        def square(i):
             rows = SIZES[i] // P
             heads = SIZES[i] // HEAD_DIM
             squares = pieces.tile([TOKENS, heads, rows, P // rows], F32, name="squares")
-            sumsq = pieces.tile([TOKENS, heads], F32, name="sumsq")
-            acc_heads = acc[:].rearrange("t (a h c) -> t h a c", a=rows, h=heads)
+            sumsq[i] = pieces.tile([TOKENS, heads], F32, name="sums_of_squares")
+            acc_heads = accs[i][:].rearrange("t (a h c) -> t h a c", a=rows, h=heads)
             for h in range(heads):
                 nc.scalar.activation(
                     out=squares[:, h],
                     in_=acc_heads[:, h],
                     func=ACT.Square,
-                    accum_out=sumsq[:, h : h + 1],
+                    accum_out=sumsq[i][:, h : h + 1],
                 )
+
+        def scale(i):
+            rows = SIZES[i] // P
+            heads = SIZES[i] // HEAD_DIM
             inv_rms = pieces.tile([TOKENS, heads], F32, name="inv_rms")
             nc.scalar.activation(
                 out=inv_rms[:],
-                in_=sumsq[:],
+                in_=sumsq[i][:],
                 func=ACT.Abs_reciprocal_sqrt,
                 scale=1.0 / HEAD_DIM,
                 bias=EPS,
             )
-            return inv_rms
-
-        def scale(i, acc, inv_rms):
-            rows = SIZES[i] // P
-            heads = SIZES[i] // HEAD_DIM
             normed = pieces.tile([TOKENS, heads, HEAD_DIM], F32, name="normed")
-            acc_by_d = acc[:].rearrange("t (a h c) -> t h c a", a=rows, h=heads)
+            acc_by_d = accs[i][:].rearrange("t (a h c) -> t h c a", a=rows, h=heads)
             for h in range(heads):
                 nc.vector.scalar_tensor_tensor(
                     out=normed[:, h, :].rearrange("t (c a) -> t c a", a=rows),
@@ -174,7 +173,6 @@ def tile_combcrossattention_pa_s_kernel(tc, hidden_states, Wq, q_norm_w, out):
         )
         hs_codes = consts.tile([P, TOKENS], U32, align_bytes=64)
         hs_scales = consts.tile([P, TOKENS], U8, align_bytes=64)
-        nc.vector.quantize_mx(out=hs_codes[:].bitcast(FP8X4), scales=hs_scales[:], in_=hs_grouped[:])
 
         gain_spread = banked.tile([P, HEAD_DIM], F32, name="gain_spread", tag="bank")
         nc.tensor.matmul(out=gain_spread[:], lhsT=ones[:], rhs=gain_row[:], start=True, stop=True)
@@ -183,29 +181,38 @@ def tile_combcrossattention_pa_s_kernel(tc, hidden_states, Wq, q_norm_w, out):
 
 
         grouped = {0: copy_out(0, banks[0])}
-        packed = {}
+        packed = {0: quantise(0, grouped[0])}
+        nc.vector.quantize_mx(out=hs_codes[:].bitcast(FP8X4), scales=hs_scales[:], in_=hs_grouped[:])
         accs = {}
-        inv = {}
+        sumsq = {}
         for i in range(1, 5):
             banks[i] = flip(i)
             grouped[i] = copy_out(i, banks[i])
-            packed[i - 1] = quantise(i - 1, grouped[i - 1])
+            if i > 1:
+                packed[i - 1] = quantise(i - 1, grouped[i - 1])
         packed[4] = quantise(4, grouped[4])
         for i in range(3):
             accs[i] = multiply(i, *packed[i])
         for i in range(5, 9):
             banks[i] = flip(i)
-        for i in range(3):
-            inv[i] = rms(i, accs[i])
-            if i < 2:
-                scale(i, accs[i], inv[i])
-        for i in range(5, 9):
-            grouped[i] = copy_out(i, banks[i])
-        scale(2, accs[2], inv[2])
-        for i in range(5, 9):
-            packed[i] = quantise(i, grouped[i])
+        square(0)
+        square(1)
+        scale(0)
+        grouped[5] = copy_out(5, banks[5])
+        square(2)
+        scale(1)
+        packed[5] = quantise(5, grouped[5])
+        grouped[6] = copy_out(6, banks[6])
+        grouped[7] = copy_out(7, banks[7])
+        packed[6] = quantise(6, grouped[6])
+        scale(2)
+        grouped[8] = copy_out(8, banks[8])
+        packed[7] = quantise(7, grouped[7])
+        packed[8] = quantise(8, grouped[8])
         for i in range(3, 9):
             accs[i] = multiply(i, *packed[i])
-        for i in range(3, 9):
-            inv[i] = rms(i, accs[i])
-            scale(i, accs[i], inv[i])
+        square(3)
+        for i in range(4, 9):
+            square(i)
+            scale(i - 1)
+        scale(8)

@@ -22,7 +22,8 @@ K_WORDS = K // 2
 HALVES = K_WORDS // P
 PACK = 4
 SIZES = 7 * [256] + 2 * [128]
-WARM_PASSES = 10
+PLAIN_WARM_PASSES = 5
+WARM_PASSES = 9
 VECTOR_PIECES = (4, 5, 7)
 
 FLOPS = 2 * TOKENS * HEADS * HEAD_DIM * K
@@ -37,6 +38,8 @@ def tile_combcrossattention_pa_s_kernel(tc, hidden_states, Wq, q_norm_w, out):
         pieces = ctx.enter_context(tc.tile_pool(name="pieces", bufs=n))
         banked = ctx.enter_context(tc.psum_pool(name="banked", bufs=8))
 
+        ones = consts.tile([P, P], BF16)
+        nc.vector.memset(ones[:], 1.0)
         idle_grouped = consts.tile([P, P * PACK], BF16, align_bytes=64)
         nc.vector.memset(idle_grouped[:].bitcast(F32), 0.0)
         idle_codes = consts.tile([P, P], U32, align_bytes=64)
@@ -64,8 +67,6 @@ def tile_combcrossattention_pa_s_kernel(tc, hidden_states, Wq, q_norm_w, out):
 
         ident = consts.tile([P, P], F32)
         masks.make_identity(nc, ident[:])
-        ones = consts.tile([P, P], BF16)
-        nc.vector.memset(ones[:], 1.0)
         one = consts.tile([P, 1], F32)
         nc.vector.memset(one[:], 1.0)
         nc.scalar.activation(out=one[:], in_=one[:], func=ACT.Abs_reciprocal_sqrt)
@@ -152,6 +153,8 @@ def tile_combcrossattention_pa_s_kernel(tc, hidden_states, Wq, q_norm_w, out):
             nc.sync.dma_start(out=out[first : first + heads].rearrange("h t d -> t h d"), in_=normed[:])
 
         ctx.enter_context(tc.manual_schedule())
+        for w in range(PLAIN_WARM_PASSES):
+            nc.tensor.matmul(out=idle_sums[:], lhsT=ones[:], rhs=ones[:], start=True, stop=True)
         for w in range(WARM_PASSES):
             nc.tensor.matmul_mx(
                 out=idle_sums[:],

@@ -23,7 +23,7 @@ HALVES = K_WORDS // P
 PACK = 4
 SIZES = 7 * [256] + 2 * [128]
 PLAIN_WARM_PASSES = 5
-WARM_PASSES = 9
+WARM_PASSES = 12
 VECTOR_PIECES = (4, 5, 7)
 
 FLOPS = 2 * TOKENS * HEADS * HEAD_DIM * K

from contextlib import ExitStack

import concourse.masks as masks
import concourse.mybir as mybir

F32 = mybir.dt.float32
BF16 = mybir.dt.bfloat16
U32 = mybir.dt.uint32
U8 = mybir.dt.uint8
FP8X4 = mybir.dt.float8_e4m3fn_x4
ACT = mybir.ActivationFunctionType
ALU = mybir.AluOpType

P = 128
TOKENS = 128
K = 512
HEADS = 16
HEAD_DIM = 128
EPS = 1e-05

K_WORDS = K // 2
HALVES = K_WORDS // P
PACK = 4
SIZES = 7 * [256] + 2 * [128]
PLAIN_WARM_PASSES = 5
WARM_PASSES = 12
VECTOR_PIECES = (4, 5, 7)

FLOPS = 2 * TOKENS * HEADS * HEAD_DIM * K


def tile_combcrossattention_pa_s_kernel(tc, hidden_states, Wq, q_norm_w, out):
    nc = tc.nc
    n = len(SIZES)
    starts = [sum(SIZES[:i]) for i in range(n)]
    with ExitStack() as ctx:
        consts = ctx.enter_context(tc.tile_pool(name="consts", bufs=1))
        pieces = ctx.enter_context(tc.tile_pool(name="pieces", bufs=n))
        banked = ctx.enter_context(tc.psum_pool(name="banked", bufs=8))

        ones = consts.tile([P, P], BF16)
        nc.vector.memset(ones[:], 1.0)
        idle_grouped = consts.tile([P, P * PACK], BF16, align_bytes=64)
        nc.vector.memset(idle_grouped[:].bitcast(F32), 0.0)
        idle_codes = consts.tile([P, P], U32, align_bytes=64)
        idle_scales = consts.tile([P, P], U8, align_bytes=64)
        nc.vector.quantize_mx(
            out=idle_codes[:].bitcast(FP8X4), scales=idle_scales[:], in_=idle_grouped[:]
        )
        idle_sums = banked.tile([P, P], F32, name="idle_sums", tag="bank")

        def load_piece(i):
            rows = SIZES[i] // P
            raw = pieces.tile([P, rows * K], BF16, name="w_raw")
            src = Wq[starts[i] : starts[i] + SIZES[i], :]
            nc.sync.dma_start(out=raw[:], in_=src.rearrange("(p a) k -> p (a k)", a=rows))
            return raw

        w_raw = [load_piece(0)]
        hs_raw = consts.tile([P, K], BF16)
        nc.sync.dma_start(out=hs_raw[:], in_=hidden_states)
        gain_row = consts.tile([P, HEAD_DIM], BF16)
        nc.vector.memset(gain_row[:], 0.0)
        nc.sync.dma_start(out=gain_row[0:1, :], in_=q_norm_w.rearrange("(o d) -> o d", o=1))
        for i in range(1, n):
            w_raw.append(load_piece(i))

        ident = consts.tile([P, P], F32)
        masks.make_identity(nc, ident[:])
        one = consts.tile([P, 1], F32)
        nc.vector.memset(one[:], 1.0)
        nc.scalar.activation(out=one[:], in_=one[:], func=ACT.Abs_reciprocal_sqrt)

        def transpose_words(dst, src_words):
            for u in range(HALVES):
                nc.tensor.transpose(dst[:, u, :], src_words[:, u::HALVES], ident[:])

        def flip(i):
            words = w_raw[i][:].bitcast(F32)
            rows = SIZES[i] // P
            bank = banked.tile([P, rows, HALVES, P], F32, name="bank", tag="bank")
            for a in range(rows):
                transpose_words(bank[:, a], words[:, a * K_WORDS : (a + 1) * K_WORDS])
            return bank

        def copy_out(i, bank):
            rows = SIZES[i] // P
            grouped = pieces.tile([P, SIZES[i] * PACK], BF16, align_bytes=64, name="grouped")
            dst = grouped[:].bitcast(F32).rearrange("p (a c u) -> p a c u", a=rows, u=HALVES)
            src = bank[:].rearrange("p a u c -> p a c u")
            if i in VECTOR_PIECES:
                nc.vector.tensor_copy(out=dst, in_=src)
            else:
                nc.scalar.copy(out=dst, in_=src)
            return grouped

        def quantise(i, grouped):
            codes = pieces.tile([P, SIZES[i]], U32, align_bytes=64, name="codes")
            scales = pieces.tile([P, SIZES[i]], U8, align_bytes=64, name="scales")
            nc.vector.quantize_mx(out=codes[:].bitcast(FP8X4), scales=scales[:], in_=grouped[:])
            return codes, scales

        def multiply(i, codes, scales):
            acc = banked.tile([TOKENS, SIZES[i]], F32, name="acc", tag="bank")
            nc.tensor.matmul_mx(
                out=acc[:],
                lhsT=hs_codes[:].bitcast(FP8X4),
                lhsT_scale=hs_scales[:],
                rhs=codes[:].bitcast(FP8X4),
                rhs_scale=scales[:],
                start=True,
                stop=True,
            )
            return acc

        def square(i):
            rows = SIZES[i] // P
            heads = SIZES[i] // HEAD_DIM
            squares = pieces.tile([TOKENS, heads, rows, P // rows], F32, name="squares")
            sumsq[i] = pieces.tile([TOKENS, heads], F32, name="sums_of_squares")
            acc_heads = accs[i][:].rearrange("t (a h c) -> t h a c", a=rows, h=heads)
            for h in range(heads):
                nc.scalar.activation(
                    out=squares[:, h],
                    in_=acc_heads[:, h],
                    func=ACT.Square,
                    accum_out=sumsq[i][:, h : h + 1],
                )

        def scale(i):
            rows = SIZES[i] // P
            heads = SIZES[i] // HEAD_DIM
            inv_rms = pieces.tile([TOKENS, heads], F32, name="inv_rms")
            nc.scalar.activation(
                out=inv_rms[:],
                in_=sumsq[i][:],
                func=ACT.Abs_reciprocal_sqrt,
                scale=1.0 / HEAD_DIM,
                bias=EPS,
            )
            normed = pieces.tile([TOKENS, heads, HEAD_DIM], F32, name="normed")
            acc_by_d = accs[i][:].rearrange("t (a h c) -> t h c a", a=rows, h=heads)
            for h in range(heads):
                nc.vector.scalar_tensor_tensor(
                    out=normed[:, h, :].rearrange("t (c a) -> t c a", a=rows),
                    in0=acc_by_d[:, h],
                    scalar=inv_rms[:, h : h + 1],
                    in1=gain[:].rearrange("t (c a) -> t c a", a=rows),
                    op0=ALU.mult,
                    op1=ALU.mult,
                )
            first = starts[i] // HEAD_DIM
            nc.sync.dma_start(out=out[first : first + heads].rearrange("h t d -> t h d"), in_=normed[:])

        ctx.enter_context(tc.manual_schedule())
        for w in range(PLAIN_WARM_PASSES):
            nc.tensor.matmul(out=idle_sums[:], lhsT=ones[:], rhs=ones[:], start=True, stop=True)
        for w in range(WARM_PASSES):
            nc.tensor.matmul_mx(
                out=idle_sums[:],
                lhsT=idle_codes[:].bitcast(FP8X4),
                lhsT_scale=idle_scales[:],
                rhs=idle_codes[:].bitcast(FP8X4),
                rhs_scale=idle_scales[:],
                start=True,
                stop=True,
            )
        banks = {0: flip(0)}

        hs_flipped = banked.tile([P, HALVES, TOKENS], F32, name="hs_flipped", tag="bank")
        transpose_words(hs_flipped, hs_raw[:].bitcast(F32))
        hs_grouped = consts.tile([P, TOKENS * PACK], BF16, align_bytes=64)
        nc.vector.tensor_copy(
            out=hs_grouped[:].bitcast(F32).rearrange("p (r u) -> p r u", u=HALVES),
            in_=hs_flipped[:].rearrange("p u r -> p r u"),
        )
        hs_codes = consts.tile([P, TOKENS], U32, align_bytes=64)
        hs_scales = consts.tile([P, TOKENS], U8, align_bytes=64)

        gain_spread = banked.tile([P, HEAD_DIM], F32, name="gain_spread", tag="bank")
        nc.tensor.matmul(out=gain_spread[:], lhsT=ones[:], rhs=gain_row[:], start=True, stop=True)
        gain = consts.tile([P, HEAD_DIM], F32)
        nc.vector.tensor_copy(out=gain[:], in_=gain_spread[:])


        grouped = {0: copy_out(0, banks[0])}
        packed = {0: quantise(0, grouped[0])}
        nc.vector.quantize_mx(out=hs_codes[:].bitcast(FP8X4), scales=hs_scales[:], in_=hs_grouped[:])
        accs = {}
        sumsq = {}
        for i in range(1, 5):
            banks[i] = flip(i)
            grouped[i] = copy_out(i, banks[i])
            if i > 1:
                packed[i - 1] = quantise(i - 1, grouped[i - 1])
        packed[4] = quantise(4, grouped[4])
        for i in range(3):
            accs[i] = multiply(i, *packed[i])
        for i in range(5, 9):
            banks[i] = flip(i)
        square(0)
        square(1)
        scale(0)
        grouped[5] = copy_out(5, banks[5])
        square(2)
        scale(1)
        packed[5] = quantise(5, grouped[5])
        grouped[6] = copy_out(6, banks[6])
        grouped[7] = copy_out(7, banks[7])
        packed[6] = quantise(6, grouped[6])
        scale(2)
        grouped[8] = copy_out(8, banks[8])
        packed[7] = quantise(7, grouped[7])
        packed[8] = quantise(8, grouped[8])
        for i in range(3, 9):
            accs[i] = multiply(i, *packed[i])
        square(3)
        for i in range(4, 9):
            square(i)
            scale(i - 1)
        scale(8)
